import numpy as np
import ml_dtypes


def mxq(x, axis, fmt="e4m3"):
    dtype, down = {"e4m3": (ml_dtypes.float8_e4m3fn, 7), "e5m2": (ml_dtypes.float8_e5m2, 14)}[fmt]
    v = np.moveaxis(np.asarray(x, np.float32).astype(ml_dtypes.bfloat16).astype(np.float64), axis, -1)
    blocks = v.reshape(v.shape[:-1] + (-1, 32))
    amax = np.abs(blocks).max(-1, keepdims=True)
    byte = np.maximum(np.where(amax > 0, np.frexp(amax)[1] - 1 + 127, 0) - down, 1)
    scale = np.exp2(byte - 127.0)
    codes = (blocks / scale).astype(np.float32).astype(dtype).astype(np.float64)
    return np.moveaxis((codes * scale).reshape(v.shape), -1, axis)


WIDE = False


def mx_kscale(k):
    if not WIDE:
        return np.ones(k)
    levels = np.array([10, -10, 5, -5, 0])
    if k % 512:
        return np.exp2(np.random.permutation(np.resize(levels, k // 32))).repeat(32)
    a = np.empty((k // 512, 16))
    for p in range(k // 512):
        a[p, :8] = np.random.permutation(np.resize(levels, 8))
        for g in range(8):
            far = levels[np.abs(levels - a[p, g]) >= 10]
            a[p, g + 8] = far[np.random.randint(len(far))]
    return np.exp2(a.ravel()).repeat(32)


BF16 = ml_dtypes.bfloat16


def bf(x):
    return np.asarray(x, np.float32).astype(BF16)


def f64(x):
    return np.asarray(x).astype(np.float64)


B, HD, NH, H, W, F = 2, 1024, 8, 16, 32, 2048
HEAD = HD // NH
P = H * W


def rms_in(x, w, eps=1e-8):
    std = np.std(x, axis=(-2, -1), keepdims=True, ddof=1)
    return x / (std + eps) * w[None, :, None, None]


def ln(x, w, b, eps=1e-5):
    mu = np.mean(x, axis=-1, keepdims=True)
    var = np.var(x, axis=-1, keepdims=True)
    return (x - mu) / np.sqrt(var + eps) * w + b


def setup_inputs():
    n = np.random.standard_normal
    s = mx_kscale(HD)
    return {"x": bf(n((B, HD, H, W)) * (0.5 + np.random.random((B, HD, 1, 1))) + 0.5 * n((B, HD, 1, 1))),
            "norm1_w": bf((1.0 + 0.1 * n(HD)) * s),
            "qkv_w": bf(n((3 * HD, HD)) / np.sqrt(HD) / s[None, :]),
            "qkv_b": bf(0.1 * n(3 * HD)),
            "qn_w": bf(1.0 + 0.1 * n(HEAD)), "qn_b": bf(0.1 * n(HEAD)),
            "kn_w": bf(1.0 + 0.1 * n(HEAD)), "kn_b": bf(0.1 * n(HEAD))}


def reference(x, norm1_w, qkv_w, qkv_b, qn_w, qn_b, kn_w, kn_b):
    h1 = rms_in(f64(x), f64(norm1_w)).reshape(B, HD, P)
    qkv = (mxq(f64(qkv_w), 1, "e4m3") @ mxq(h1, 1, "e4m3")) + f64(qkv_b)[None, :, None]
    t = qkv.reshape(B, NH, 3 * HEAD, H, W).transpose(0, 1, 3, 4, 2)
    q, k, v = np.split(t, 3, axis=-1)
    q = ln(q, f64(qn_w), f64(qn_b))
    k = ln(k, f64(kn_w), f64(kn_b))
    return q, k, np.ascontiguousarray(v)

@@ -1,0 +1,391 @@
+from contextlib import ExitStack
+
+import concourse.masks as masks
+import concourse.mybir as mybir
+
+F32 = mybir.dt.float32
+BF16 = mybir.dt.bfloat16
+U32 = mybir.dt.uint32
+U8 = mybir.dt.uint8
+I32 = mybir.dt.int32
+FP8X4 = mybir.dt.float8_e4m3fn_x4
+ALU = mybir.AluOpType
+ACT = mybir.ActivationFunctionType
+
+P = 128
+FLOPS = 2 * 3072 * 1024 * 1024
+MANUAL = False
+
+Q0, K0, Q1, K1, V0, V1 = (0, 0), (1, 0), (0, 1), (1, 1), (2, 0), (2, 1)
+LOAD_ORDER = (Q0, K0, Q1, K1, V0, V1)
+QK_UNITS = ((Q0, 0), (K0, 0), (Q1, 0), (K1, 0), (Q0, 1), (K0, 1), (Q1, 1), (K1, 1))
+
+
+def tile_axialattentionblock_pa_kernel(
+    tc, x, norm1_w, qkv_w, qkv_b, qn_w, qn_b, kn_w, kn_b, out_0, out_1, out_2
+):
+    nc = tc.nc
+    outs = (out_0, out_1, out_2)
+    with ExitStack() as ctx:
+        const = ctx.enter_context(tc.tile_pool(name="const", bufs=1))
+        wgp = ctx.enter_context(tc.tile_pool(name="wgp", bufs=3))
+        hgp = ctx.enter_context(tc.tile_pool(name="hgp", bufs=2))
+        small = ctx.enter_context(tc.tile_pool(name="small", bufs=4))
+        zp = ctx.enter_context(tc.tile_pool(name="zp", bufs=12))
+        op = ctx.enter_context(tc.tile_pool(name="op", bufs=3))
+        vp = ctx.enter_context(tc.tile_pool(name="vp", bufs=2))
+        jp = ctx.enter_context(tc.tile_pool(name="jp", bufs=2))
+        psc = ctx.enter_context(tc.psum_pool(name="psc", bufs=1))
+        psx = ctx.enter_context(tc.psum_pool(name="psx", bufs=4))
+        psa = ctx.enter_context(tc.psum_pool(name="psa", bufs=3))
+        if MANUAL:
+            ctx.enter_context(tc.manual_schedule())
+
+        x_sb = const.tile([P, 2, 2, 2048], BF16, name="x_sb")
+        b_bc = const.tile([P, 8, 3, P], BF16, name="b_bc")
+        w_view = qkv_w.rearrange("(n t p) k -> t p n k", t=3, p=P)
+        wraw = {}
+
+        def load_x(b, g):
+            nc.sync.dma_start(
+                out=x_sb[:, b, g, :],
+                in_=x[b].rearrange("(g q t) h w -> g q (t h w)", g=2, t=4)[g],
+            )
+
+        def load_w(chunk):
+            kind, half = chunk
+            wr = const.tile([P, 4, 1024], BF16, name="wraw%d%d" % chunk)
+            nc.sync.dma_start(out=wr[:], in_=w_view[kind, :, 4 * half : 4 * half + 4, :])
+            wraw[chunk] = wr
+
+        load_x(0, 0)
+        load_x(0, 1)
+        load_w(Q0)
+        load_w(K0)
+        nc.sync.dma_start(
+            out=b_bc[:].rearrange("q n t c -> q (n t c)"), in_=qkv_b.partition_broadcast(P)
+        )
+        load_w(Q1)
+        load_w(K1)
+        load_x(1, 0)
+        load_x(1, 1)
+        load_w(V0)
+        load_w(V1)
+
+        wrow = const.tile([P, 512], BF16, name="wrow")
+        nc.vector.memset(wrow[:].bitcast(I32), 0)
+        for k, vec in enumerate((qn_w, kn_w, qn_b, kn_b)):
+            nc.scalar.dma_start(
+                out=wrow[0:1, P * k : P * (k + 1)], in_=vec.rearrange("(o n) -> o n", o=1)
+            )
+        nw = const.tile([P, 8], BF16, name="nw")
+        with nc.allow_non_contiguous_dma(reason="1024 gains, four to a piece"):
+            nc.scalar.dma_start(
+                out=nw[:].rearrange("q (g t) -> q g t", t=4),
+                in_=norm1_w.rearrange("(g q t) -> q g t", g=2, t=4),
+            )
+
+        ones = const.tile([P, P], BF16, name="ones")
+        nc.vector.memset(ones[:], 1.0)
+        one1 = const.tile([P, 1], F32, name="one1")
+        nc.vector.memset(one1[:], 1.0)
+        eps = const.tile([P, 1], F32, name="eps")
+        nc.vector.memset(eps[:], 1e-5)
+        warm = const.tile([P, 1], F32, name="warm")
+        nc.scalar.activation(out=warm[:], in_=one1[:], func=ACT.Sqrt)
+        ident = const.tile([P, P], F32, name="ident")
+        masks.make_identity(nc, ident[:])
+
+        lnc = psc.tile([P, 512], F32, name="lnc")
+        nc.tensor.matmul(out=lnc[:], lhsT=ones[:], rhs=wrow[:], start=True, stop=True)
+
+        st = const.tile([P, 2, 8, 6], F32, name="st")
+        xsc = {}
+        hgs = {}
+        hc = {}
+        hs = {}
+
+        def x_stats(b):
+            for s in range(8):
+                g, t = divmod(s, 4)
+                nc.vector.bn_stats(out=st[:, b, s, :], in_=x_sb[:, b, g, 512 * t : 512 * (t + 1)])
+
+        def x_small(b):
+            d = small.tile([P, 8], F32, name="xd")
+            nc.vector.tensor_tensor(out=d[:], in0=st[:, b, :, 1], in1=st[:, b, :, 4], op=ALU.subtract)
+            d2 = small.tile([P, 8], F32, name="xd2")
+            nc.vector.tensor_tensor(out=d2[:], in0=d[:], in1=d[:], op=ALU.mult)
+            m2 = small.tile([P, 8], F32, name="xm2")
+            nc.vector.tensor_tensor(out=m2[:], in0=st[:, b, :, 2], in1=st[:, b, :, 5], op=ALU.add)
+            ss = small.tile([P, 8], F32, name="xss")
+            nc.vector.scalar_tensor_tensor(
+                out=ss[:], in0=d2[:], scalar=128.0, in1=m2[:], op0=ALU.mult, op1=ALU.add
+            )
+            sd = small.tile([P, 8], F32, name="xsd")
+            nc.scalar.activation(out=sd[:], in_=ss[:], func=ACT.Sqrt, scale=1.0 / 511.0)
+            den = small.tile([P, 8], F32, name="xden")
+            nc.vector.tensor_scalar_add(out=den[:], in0=sd[:], scalar1=1e-8)
+            rec = small.tile([P, 8], F32, name="xrec")
+            nc.vector.reciprocal(out=rec[:], in_=den[:])
+            sc = small.tile([P, 8], F32, name="xsc")
+            nc.vector.tensor_tensor(out=sc[:], in0=rec[:], in1=nw[:], op=ALU.mult)
+            xsc[b] = sc
+
+        def x_scale(b, g):
+            hg = hgp.tile([P, 2048], BF16, name="hg", align_bytes=64)
+            nc.vector.tensor_tensor(
+                out=hg[:].rearrange("q (i p t) -> q i p t", i=4, t=4),
+                in0=x_sb[:, b, g, :].rearrange("q (t p i) -> q i p t", t=4, i=4),
+                in1=xsc[b][:, 4 * g : 4 * g + 4].unsqueeze(1).unsqueeze(1).to_broadcast([P, 4, P, 4]),
+                op=ALU.mult,
+            )
+            hgs[(b, g)] = hg
+
+        def x_quant(b, g):
+            codes = const.tile([P, 512], U32, name="hc%d%d" % (b, g), align_bytes=64)
+            scales = const.tile([P, 512], U8, name="hs%d%d" % (b, g), align_bytes=64)
+            nc.vector.quantize_mx(out=codes[:].bitcast(FP8X4), scales=scales[:], in_=hgs[(b, g)][:])
+            hc[(b, g)] = codes
+            hs[(b, g)] = scales
+
+        wgs = {}
+        wc = {}
+        ws = {}
+
+        def w_turn(chunk):
+            wrf = wraw[chunk][:].bitcast(F32)
+            wg = wgp.tile([P, 2, 2048], BF16, name="wg", align_bytes=64)
+            wgf = wg[:].bitcast(F32)
+            for g in range(2):
+                for h in range(2):
+                    tp = psx.tile([P, 2, 2, P], F32, tag="aux", name="tp")
+                    for u in range(2):
+                        for nn in range(2):
+                            c0 = 2 * P * g + u
+                            nc.tensor.transpose(
+                                out=tp[:, u, nn, :],
+                                in_=wrf[:, 2 * h + nn, c0 : 2 * P * (g + 1) : 2],
+                                identity=ident[:],
+                            )
+                    nc.scalar.copy(
+                        out=wgf[:, g, 512 * h : 512 * (h + 1)].rearrange("q (o u) -> q o u", u=2),
+                        in_=tp[:].rearrange("q u n p -> q (n p) u"),
+                    )
+            wgs[chunk] = wg
+            wc[chunk] = const.tile([P, 2, 512], U32, name="wc%d%d" % chunk, align_bytes=64)
+            ws[chunk] = const.tile([P, 2, 512], U8, name="ws%d%d" % chunk, align_bytes=64)
+
+        def w_quant(chunk, g):
+            nc.vector.quantize_mx(
+                out=wc[chunk][:, g, :].bitcast(FP8X4),
+                scales=ws[chunk][:, g, :],
+                in_=wgs[chunk][:, g, :],
+            )
+
+        def product(acc, chunk, b, i):
+            for g in range(2):
+                nc.tensor.matmul_mx(
+                    out=acc[:],
+                    lhsT=hc[(b, g)][:, P * i : P * (i + 1)].bitcast(FP8X4),
+                    lhsT_scale=hs[(b, g)][:, P * i : P * (i + 1)],
+                    rhs=wc[chunk][:, g, :].bitcast(FP8X4),
+                    rhs_scale=ws[chunk][:, g, :],
+                    start=(g == 0),
+                    stop=(g == 1),
+                )
+
+        def bias_of(chunk):
+            kind, half = chunk
+            return b_bc[:, 4 * half : 4 * half + 4, kind, :]
+
+        def store(chunk, b, tile_):
+            kind, half = chunk
+            nc.sync.dma_start(
+                out=outs[kind][b, 4 * half : 4 * half + 4].rearrange("n h (w i) c -> (h w) n (i c)", i=4),
+                in_=tile_[:].rearrange("q n i c -> q n (i c)"),
+            )
+
+        def v_unit(chunk, b):
+            vst = vp.tile([P, 4, 4, P], F32, name="vst")
+            for i in range(4):
+                acc = psx.tile([P, 512], F32, tag="aux", name="vacc")
+                product(acc, chunk, b, i)
+                nc.vector.tensor_tensor(
+                    out=vst[:, :, i, :],
+                    in0=acc[:].rearrange("q (n c) -> q n c", c=P),
+                    in1=bias_of(chunk),
+                    op=ALU.add,
+                )
+            store(chunk, b, vst)
+
+        sumb = const.tile([P, 16], F32, name="sumb")
+        nsb = const.tile([P, 16], F32, name="nsb")
+
+        def bias_sums():
+            for kind in range(2):
+                for n in range(8):
+                    junk = jp.tile([P, P], F32, name="junk")
+                    nc.scalar.activation(
+                        out=junk[:],
+                        in_=b_bc[:, n, kind, :],
+                        func=ACT.Identity,
+                        accum_out=sumb[:, 8 * kind + n : 8 * kind + n + 1],
+                    )
+            nc.vector.tensor_scalar_mul(out=nsb[:], in0=sumb[:], scalar1=-1.0 / 128.0)
+
+        S = {}
+
+        def stage_e(p):
+            chunk, b = QK_UNITS[p]
+            su = small.tile([P, 16], F32, name="su")
+            zs = []
+            for i in range(4):
+                acc = psa.tile([P, 512], F32, name="acc")
+                product(acc, chunk, b, i)
+                z = zp.tile([P, 512], F32, name="z")
+                for n in range(4):
+                    nc.scalar.activation(
+                        out=z[:, P * n : P * (n + 1)],
+                        in_=acc[:, P * n : P * (n + 1)],
+                        func=ACT.Identity,
+                        accum_out=su[:, 4 * i + n : 4 * i + n + 1],
+                    )
+                nc.gpsimd.tensor_tensor(
+                    out=z[:].rearrange("q (n c) -> q n c", c=P),
+                    in0=z[:].rearrange("q (n c) -> q n c", c=P),
+                    in1=bias_of(chunk),
+                    op=ALU.add,
+                )
+                zs.append(z)
+            S[p] = {"su": su, "zs": zs}
+
+        def stage_n(p):
+            (kind, half), b = QK_UNITS[p]
+            negm = small.tile([P, 16], F32, name="negm")
+            c0 = 8 * kind + 4 * half
+            nc.vector.scalar_tensor_tensor(
+                out=negm[:].rearrange("q (i n) -> q i n", n=4),
+                in0=S[p]["su"][:].rearrange("q (i n) -> q i n", n=4),
+                scalar=-1.0 / 128.0,
+                in1=nsb[:, c0 : c0 + 4].unsqueeze(1).to_broadcast([P, 4, 4]),
+                op0=ALU.mult,
+                op1=ALU.add,
+            )
+            S[p]["negm"] = negm
+
+        def stage_ms(p):
+            negm = S[p]["negm"]
+            ssq = small.tile([P, 16], F32, name="ssq")
+            for i in range(4):
+                for n in range(4):
+                    k = 4 * i + n
+                    junk = jp.tile([P, P], F32, name="junk")
+                    nc.scalar.activation(
+                        out=junk[:],
+                        in_=S[p]["zs"][i][:, P * n : P * (n + 1)],
+                        func=ACT.Square,
+                        bias=negm[:, k : k + 1],
+                        accum_out=ssq[:, k : k + 1],
+                    )
+            sd = small.tile([P, 16], F32, name="sd")
+            nc.scalar.activation(out=sd[:], in_=ssq[:], func=ACT.Sqrt, bias=eps[:], scale=1.0 / 128.0)
+            S[p]["sd"] = sd
+
+        def stage_mv(p):
+            (kind, half), b = QK_UNITS[p]
+            negm = S[p]["negm"]
+            ost = op.tile([P, 4, 4, P], F32, name="ost")
+            for i in range(4):
+                for n in range(4):
+                    k = 4 * i + n
+                    nc.vector.scalar_tensor_tensor(
+                        out=ost[:, n, i, :],
+                        in0=S[p]["zs"][i][:, P * n : P * (n + 1)],
+                        scalar=negm[:, k : k + 1],
+                        in1=lnc[:, P * kind : P * (kind + 1)],
+                        op0=ALU.add,
+                        op1=ALU.mult,
+                    )
+            S[p]["ost"] = ost
+
+        def stage_f(p, by_head):
+            chunk, b = QK_UNITS[p]
+            kind, half = chunk
+            ost = S[p]["ost"]
+            rs = small.tile([P, 16], F32, name="rs")
+            nc.vector.reciprocal(out=rs[:], in_=S[p]["sd"][:])
+            for n in range(4):
+                for i in range(4):
+                    k = 4 * i + n
+                    nc.vector.scalar_tensor_tensor(
+                        out=ost[:, n, i, :],
+                        in0=ost[:, n, i, :],
+                        scalar=rs[:, k : k + 1],
+                        in1=lnc[:, 256 + P * kind : 256 + P * (kind + 1)],
+                        op0=ALU.mult,
+                        op1=ALU.add,
+                    )
+                if by_head:
+                    nc.sync.dma_start(
+                        out=outs[kind][b, 4 * half + n].rearrange("h (w i) c -> (h w) (i c)", i=4),
+                        in_=ost[:, n].rearrange("q i c -> q (i c)"),
+                    )
+            if not by_head:
+                store(chunk, b, ost)
+
+        x_stats(0)
+        x_small(0)
+        w_turn(Q0)
+        x_scale(0, 0)
+        w_quant(Q0, 0)
+        x_quant(0, 0)
+        x_scale(0, 1)
+        w_quant(Q0, 1)
+        x_quant(0, 1)
+        w_turn(K0)
+        bias_sums()
+        w_quant(K0, 0)
+        w_quant(K0, 1)
+        w_turn(Q1)
+
+        def filler(p):
+            if p == 0:
+                w_turn(K1)
+                w_quant(Q1, 0)
+                w_quant(Q1, 1)
+                x_stats(1)
+                x_small(1)
+            elif p == 1:
+                w_turn(V0)
+                x_scale(1, 0)
+                w_quant(K1, 0)
+                w_quant(K1, 1)
+                x_quant(1, 0)
+            elif p == 2:
+                w_turn(V1)
+                x_scale(1, 1)
+                w_quant(V0, 0)
+                w_quant(V0, 1)
+                x_quant(1, 1)
+            elif p == 3:
+                w_quant(V1, 0)
+                w_quant(V1, 1)
+                v_unit(V0, 0)
+            elif p == 4:
+                v_unit(V1, 0)
+            elif p == 5:
+                v_unit(V0, 1)
+            elif p == 6:
+                v_unit(V1, 1)
+
+        for p in range(10):
+            if p < 8:
+                stage_e(p)
+            if 0 <= p - 2 < 8:
+                stage_f(p - 2, p - 2 == 7)
+            if 0 <= p - 1 < 8:
+                stage_mv(p - 1)
+                stage_ms(p - 1)
+            if p < 8:
+                stage_n(p)
+            filler(p)

@@ -111,24 +111,27 @@ def tile_axialattentionblock_pa_kernel(
                 nc.vector.bn_stats(out=st[:, b, s, :], in_=x_sb[:, b, g, 512 * t : 512 * (t + 1)])
 
         def x_small(b):
+            eng = nc.vector if b == 0 else nc.gpsimd
             d = small.tile([P, 8], F32, name="xd")
-            nc.vector.tensor_tensor(out=d[:], in0=st[:, b, :, 1], in1=st[:, b, :, 4], op=ALU.subtract)
+            eng.tensor_tensor(out=d[:], in0=st[:, b, :, 1], in1=st[:, b, :, 4], op=ALU.subtract)
             d2 = small.tile([P, 8], F32, name="xd2")
-            nc.vector.tensor_tensor(out=d2[:], in0=d[:], in1=d[:], op=ALU.mult)
+            eng.tensor_tensor(out=d2[:], in0=d[:], in1=d[:], op=ALU.mult)
             m2 = small.tile([P, 8], F32, name="xm2")
-            nc.vector.tensor_tensor(out=m2[:], in0=st[:, b, :, 2], in1=st[:, b, :, 5], op=ALU.add)
-            ss = small.tile([P, 8], F32, name="xss")
-            nc.vector.scalar_tensor_tensor(
-                out=ss[:], in0=d2[:], scalar=128.0, in1=m2[:], op0=ALU.mult, op1=ALU.add
+            eng.tensor_tensor(out=m2[:], in0=st[:, b, :, 2], in1=st[:, b, :, 5], op=ALU.add)
+            d3 = small.tile([P, 8], F32, name="xd3")
+            eng.tensor_scalar(
+                out=d3[:], in0=d2[:], scalar1=128.0, scalar2=0.0, op0=ALU.mult, op1=ALU.add
             )
+            ss = small.tile([P, 8], F32, name="xss")
+            eng.tensor_tensor(out=ss[:], in0=d3[:], in1=m2[:], op=ALU.add)
             sd = small.tile([P, 8], F32, name="xsd")
             nc.scalar.activation(out=sd[:], in_=ss[:], func=ACT.Sqrt, scale=1.0 / 511.0)
             den = small.tile([P, 8], F32, name="xden")
-            nc.vector.tensor_scalar_add(out=den[:], in0=sd[:], scalar1=1e-8)
+            eng.tensor_scalar_add(out=den[:], in0=sd[:], scalar1=1e-8)
             rec = small.tile([P, 8], F32, name="xrec")
             nc.vector.reciprocal(out=rec[:], in_=den[:])
             sc = small.tile([P, 8], F32, name="xsc")
-            nc.vector.tensor_tensor(out=sc[:], in0=rec[:], in1=nw[:], op=ALU.mult)
+            eng.tensor_tensor(out=sc[:], in0=rec[:], in1=nw[:], op=ALU.mult)
             xsc[b] = sc
 
         def x_scale(b, g):
@@ -263,13 +266,20 @@ def tile_axialattentionblock_pa_kernel(
             (kind, half), b = QK_UNITS[p]
             negm = small.tile([P, 16], F32, name="negm")
             c0 = 8 * kind + 4 * half
-            nc.vector.scalar_tensor_tensor(
-                out=negm[:].rearrange("q (i n) -> q i n", n=4),
-                in0=S[p]["su"][:].rearrange("q (i n) -> q i n", n=4),
-                scalar=-1.0 / 128.0,
-                in1=nsb[:, c0 : c0 + 4].unsqueeze(1).to_broadcast([P, 4, 4]),
+            negs = small.tile([P, 16], F32, name="negs")
+            nc.gpsimd.tensor_scalar(
+                out=negs[:],
+                in0=S[p]["su"][:],
+                scalar1=-1.0 / 128.0,
+                scalar2=0.0,
                 op0=ALU.mult,
                 op1=ALU.add,
+            )
+            nc.gpsimd.tensor_tensor(
+                out=negm[:].rearrange("q (i n) -> q i n", n=4),
+                in0=negs[:].rearrange("q (i n) -> q i n", n=4),
+                in1=nsb[:, c0 : c0 + 4].unsqueeze(1).to_broadcast([P, 4, 4]),
+                op=ALU.add,
             )
             S[p]["negm"] = negm
 

@@ -14,7 +14,6 @@ ACT = mybir.ActivationFunctionType
 
 P = 128
 FLOPS = 2 * 3072 * 1024 * 1024
-MANUAL = False
 
 Q0, K0, Q1, K1, V0, V1 = (0, 0), (1, 0), (0, 1), (1, 1), (2, 0), (2, 1)
 LOAD_ORDER = (Q0, K0, Q1, K1, V0, V1)
@@ -38,18 +37,15 @@ def tile_axialattentionblock_pa_kernel(
         psc = ctx.enter_context(tc.psum_pool(name="psc", bufs=1))
         psx = ctx.enter_context(tc.psum_pool(name="psx", bufs=4))
         psa = ctx.enter_context(tc.psum_pool(name="psa", bufs=3))
-        if MANUAL:
-            ctx.enter_context(tc.manual_schedule())
 
         x_sb = const.tile([P, 2, 2, 2048], BF16, name="x_sb")
-        b_bc = const.tile([P, 8, 3, P], BF16, name="b_bc")
         w_view = qkv_w.rearrange("(n t p) k -> t p n k", t=3, p=P)
         wraw = {}
 
-        def load_x(b, g):
+        def load_x(b, g, lo, hi):
             nc.sync.dma_start(
-                out=x_sb[:, b, g, :],
-                in_=x[b].rearrange("(g q t) h w -> g q (t h w)", g=2, t=4)[g],
+                out=x_sb[:, b, g, 512 * lo : 512 * hi],
+                in_=x[b].rearrange("(g q t) h w -> g q (t h w)", g=2, t=4)[g][:, 512 * lo : 512 * hi],
             )
 
         def load_w(chunk):
@@ -58,26 +54,29 @@ def tile_axialattentionblock_pa_kernel(
             nc.sync.dma_start(out=wr[:], in_=w_view[kind, :, 4 * half : 4 * half + 4, :])
             wraw[chunk] = wr
 
-        load_x(0, 0)
-        load_x(0, 1)
+        for g in range(2):
+            for lo in (0, 2):
+                load_x(0, g, lo, lo + 2)
         load_w(Q0)
         load_w(K0)
-        nc.sync.dma_start(
-            out=b_bc[:].rearrange("q n t c -> q (n t c)"), in_=qkv_b.partition_broadcast(P)
-        )
         load_w(Q1)
         load_w(K1)
-        load_x(1, 0)
-        load_x(1, 1)
+        load_x(1, 0, 0, 4)
+        load_x(1, 1, 0, 4)
         load_w(V0)
         load_w(V1)
 
-        wrow = const.tile([P, 512], BF16, name="wrow")
-        nc.vector.memset(wrow[:].bitcast(I32), 0)
-        for k, vec in enumerate((qn_w, kn_w, qn_b, kn_b)):
-            nc.scalar.dma_start(
-                out=wrow[0:1, P * k : P * (k + 1)], in_=vec.rearrange("(o n) -> o n", o=1)
-            )
+        one1 = const.tile([P, 1], F32, name="one1")
+        nc.vector.memset(one1[:], 1.0)
+        eps = const.tile([P, 1], F32, name="eps")
+        nc.vector.memset(eps[:], 1e-5)
+        warm = const.tile([P, 1], F32, name="warm")
+        nc.scalar.activation(out=warm[:], in_=one1[:], func=ACT.Sqrt)
+        vec = const.tile([P, P], BF16, name="vec")
+        nc.vector.memset(vec[:].bitcast(I32), 0)
+        nc.scalar.dma_start(out=vec[0:24, :], in_=qkv_b.rearrange("(r c) -> r c", c=P))
+        for r, v in enumerate((qn_w, kn_w, qn_b, kn_b)):
+            nc.scalar.dma_start(out=vec[24 + r : 25 + r, :], in_=v.rearrange("(o n) -> o n", o=1))
         nw = const.tile([P, 8], BF16, name="nw")
         with nc.allow_non_contiguous_dma(reason="1024 gains, four to a piece"):
             nc.scalar.dma_start(
@@ -85,19 +84,46 @@ def tile_axialattentionblock_pa_kernel(
                 in_=norm1_w.rearrange("(g q t) -> q g t", g=2, t=4),
             )
 
-        ones = const.tile([P, P], BF16, name="ones")
-        nc.vector.memset(ones[:], 1.0)
-        one1 = const.tile([P, 1], F32, name="one1")
-        nc.vector.memset(one1[:], 1.0)
-        eps = const.tile([P, 1], F32, name="eps")
-        nc.vector.memset(eps[:], 1e-5)
-        warm = const.tile([P, 1], F32, name="warm")
-        nc.scalar.activation(out=warm[:], in_=one1[:], func=ACT.Sqrt)
         ident = const.tile([P, P], F32, name="ident")
         masks.make_identity(nc, ident[:])
+        ident_b = const.tile([P, P], BF16, name="ident_b")
+        nc.gpsimd.tensor_copy(out=ident_b[:], in_=ident[:])
+
+        def spread(out, eye, r, rows):
+            nc.tensor.matmul(
+                out=out, lhsT=eye[:, r : r + 1].to_broadcast([P, P]), rhs=rows[:], start=True, stop=True
+            )
 
         lnc = psc.tile([P, 512], F32, name="lnc")
-        nc.tensor.matmul(out=lnc[:], lhsT=ones[:], rhs=wrow[:], start=True, stop=True)
+        b_qk = const.tile([P, 2, 8, P], F32, name="b_qk")
+        b_v = const.tile([P, 8, P], F32, name="b_v")
+
+        vecm = const.tile([P, P], F32, name="vecm")
+
+        def centre():
+            rowsum = small.tile([P, 1], F32, name="rowsum")
+            nc.vector.reduce_sum(out=rowsum[:], in_=vec[:], axis=mybir.AxisListType.X)
+            rowmean = small.tile([P, 1], F32, name="rowmean")
+            nc.vector.tensor_scalar_mul(out=rowmean[:], in0=rowsum[:], scalar1=-1.0 / 128.0)
+            nc.vector.tensor_scalar_add(out=vecm[:], in0=vec[:], scalar1=rowmean[:])
+
+        def ln_vectors():
+            for k in range(4):
+                spread(lnc[:, P * k : P * (k + 1)], ident_b, 24 + k, vec)
+
+        def qk_vectors(chunk):
+            kind, h = chunk
+            qb = psx.tile([P, 4, P], F32, tag="aux", name="qb")
+            for n in range(4):
+                spread(qb[:, n, :], ident, 3 * (4 * h + n) + kind, vecm)
+            nc.scalar.copy(out=b_qk[:, kind, 4 * h : 4 * h + 4, :], in_=qb[:])
+
+        def v_vectors():
+            for h in range(2):
+                vb = psx.tile([P, 4, P], F32, tag="aux", name="vb")
+                for n in range(4):
+                    spread(vb[:, n, :], ident_b, 3 * (4 * h + n) + 2, vec)
+                nc.scalar.copy(out=b_v[:, 4 * h : 4 * h + 4, :], in_=vb[:])
 
         st = const.tile([P, 2, 8, 6], F32, name="st")
         xsc = {}
@@ -105,51 +131,47 @@ def tile_axialattentionblock_pa_kernel(
         hc = {}
         hs = {}
 
+        mv = const.tile([P, 2, 8, 2], F32, name="mv")
+
         def x_stats(b):
             for s in range(8):
                 g, t = divmod(s, 4)
                 nc.vector.bn_stats(out=st[:, b, s, :], in_=x_sb[:, b, g, 512 * t : 512 * (t + 1)])
+            for s in range(8):
+                nc.vector.bn_aggr(out=mv[:, b, s, :], in_=st[:, b, s, :])
 
         def x_small(b):
-            eng = nc.vector if b == 0 else nc.gpsimd
-            d = small.tile([P, 8], F32, name="xd")
-            eng.tensor_tensor(out=d[:], in0=st[:, b, :, 1], in1=st[:, b, :, 4], op=ALU.subtract)
-            d2 = small.tile([P, 8], F32, name="xd2")
-            eng.tensor_tensor(out=d2[:], in0=d[:], in1=d[:], op=ALU.mult)
-            m2 = small.tile([P, 8], F32, name="xm2")
-            eng.tensor_tensor(out=m2[:], in0=st[:, b, :, 2], in1=st[:, b, :, 5], op=ALU.add)
-            d3 = small.tile([P, 8], F32, name="xd3")
-            eng.tensor_scalar(
-                out=d3[:], in0=d2[:], scalar1=128.0, scalar2=0.0, op0=ALU.mult, op1=ALU.add
-            )
-            ss = small.tile([P, 8], F32, name="xss")
-            eng.tensor_tensor(out=ss[:], in0=d3[:], in1=m2[:], op=ALU.add)
             sd = small.tile([P, 8], F32, name="xsd")
-            nc.scalar.activation(out=sd[:], in_=ss[:], func=ACT.Sqrt, scale=1.0 / 511.0)
+            nc.scalar.activation(out=sd[:], in_=mv[:, b, :, 1], func=ACT.Sqrt, scale=512.0 / 511.0)
             den = small.tile([P, 8], F32, name="xden")
-            eng.tensor_scalar_add(out=den[:], in0=sd[:], scalar1=1e-8)
+            nc.vector.tensor_scalar_add(out=den[:], in0=sd[:], scalar1=1e-8)
             rec = small.tile([P, 8], F32, name="xrec")
             nc.vector.reciprocal(out=rec[:], in_=den[:])
             sc = small.tile([P, 8], F32, name="xsc")
-            eng.tensor_tensor(out=sc[:], in0=rec[:], in1=nw[:], op=ALU.mult)
+            nc.vector.tensor_tensor(out=sc[:], in0=rec[:], in1=nw[:], op=ALU.mult)
             xsc[b] = sc
 
         def x_scale(b, g):
-            hg = hgp.tile([P, 2048], BF16, name="hg", align_bytes=64)
+            if g == 0:
+                hgs[b] = hgp.tile([P, 2, 2048], BF16, name="hg", align_bytes=64)
+                hc[b] = const.tile([P, 2, 512], U32, name="hc%d" % b, align_bytes=64)
+                hs[b] = const.tile([P, 2, 512], U8, name="hs%d" % b, align_bytes=64)
             nc.vector.tensor_tensor(
-                out=hg[:].rearrange("q (i p t) -> q i p t", i=4, t=4),
+                out=hgs[b][:, g, :].rearrange("q (i p t) -> q i p t", i=4, t=4),
                 in0=x_sb[:, b, g, :].rearrange("q (t p i) -> q i p t", t=4, i=4),
                 in1=xsc[b][:, 4 * g : 4 * g + 4].unsqueeze(1).unsqueeze(1).to_broadcast([P, 4, P, 4]),
                 op=ALU.mult,
             )
-            hgs[(b, g)] = hg
 
-        def x_quant(b, g):
-            codes = const.tile([P, 512], U32, name="hc%d%d" % (b, g), align_bytes=64)
-            scales = const.tile([P, 512], U8, name="hs%d%d" % (b, g), align_bytes=64)
-            nc.vector.quantize_mx(out=codes[:].bitcast(FP8X4), scales=scales[:], in_=hgs[(b, g)][:])
-            hc[(b, g)] = codes
-            hs[(b, g)] = scales
+        def quant(codes, scales, grouped, lo, hi):
+            nc.vector.quantize_mx(
+                out=codes[:, lo:hi, :].rearrange("q g w -> q (g w)").bitcast(FP8X4),
+                scales=scales[:, lo:hi, :].rearrange("q g w -> q (g w)"),
+                in_=grouped[:, lo:hi, :].rearrange("q g w -> q (g w)"),
+            )
+
+        def x_quant(b, lo, hi):
+            quant(hc[b], hs[b], hgs[b], lo, hi)
 
         wgs = {}
         wc = {}
@@ -178,28 +200,20 @@ def tile_axialattentionblock_pa_kernel(
             wc[chunk] = const.tile([P, 2, 512], U32, name="wc%d%d" % chunk, align_bytes=64)
             ws[chunk] = const.tile([P, 2, 512], U8, name="ws%d%d" % chunk, align_bytes=64)
 
-        def w_quant(chunk, g):
-            nc.vector.quantize_mx(
-                out=wc[chunk][:, g, :].bitcast(FP8X4),
-                scales=ws[chunk][:, g, :],
-                in_=wgs[chunk][:, g, :],
-            )
+        def w_quant(chunk, lo, hi):
+            quant(wc[chunk], ws[chunk], wgs[chunk], lo, hi)
 
         def product(acc, chunk, b, i):
             for g in range(2):
                 nc.tensor.matmul_mx(
                     out=acc[:],
-                    lhsT=hc[(b, g)][:, P * i : P * (i + 1)].bitcast(FP8X4),
-                    lhsT_scale=hs[(b, g)][:, P * i : P * (i + 1)],
+                    lhsT=hc[b][:, g, P * i : P * (i + 1)].bitcast(FP8X4),
+                    lhsT_scale=hs[b][:, g, P * i : P * (i + 1)],
                     rhs=wc[chunk][:, g, :].bitcast(FP8X4),
                     rhs_scale=ws[chunk][:, g, :],
                     start=(g == 0),
                     stop=(g == 1),
                 )
-
-        def bias_of(chunk):
-            kind, half = chunk
-            return b_bc[:, 4 * half : 4 * half + 4, kind, :]
 
         def store(chunk, b, tile_):
             kind, half = chunk
@@ -216,25 +230,10 @@ def tile_axialattentionblock_pa_kernel(
                 nc.vector.tensor_tensor(
                     out=vst[:, :, i, :],
                     in0=acc[:].rearrange("q (n c) -> q n c", c=P),
-                    in1=bias_of(chunk),
+                    in1=b_v[:, 4 * chunk[1] : 4 * chunk[1] + 4, :],
                     op=ALU.add,
                 )
             store(chunk, b, vst)
-
-        sumb = const.tile([P, 16], F32, name="sumb")
-        nsb = const.tile([P, 16], F32, name="nsb")
-
-        def bias_sums():
-            for kind in range(2):
-                for n in range(8):
-                    junk = jp.tile([P, P], F32, name="junk")
-                    nc.scalar.activation(
-                        out=junk[:],
-                        in_=b_bc[:, n, kind, :],
-                        func=ACT.Identity,
-                        accum_out=sumb[:, 8 * kind + n : 8 * kind + n + 1],
-                    )
-            nc.vector.tensor_scalar_mul(out=nsb[:], in0=sumb[:], scalar1=-1.0 / 128.0)
 
         S = {}
 
@@ -256,30 +255,16 @@ def tile_axialattentionblock_pa_kernel(
                 nc.gpsimd.tensor_tensor(
                     out=z[:].rearrange("q (n c) -> q n c", c=P),
                     in0=z[:].rearrange("q (n c) -> q n c", c=P),
-                    in1=bias_of(chunk),
+                    in1=b_qk[:, chunk[0], 4 * chunk[1] : 4 * chunk[1] + 4, :],
                     op=ALU.add,
                 )
                 zs.append(z)
             S[p] = {"su": su, "zs": zs}
 
         def stage_n(p):
-            (kind, half), b = QK_UNITS[p]
             negm = small.tile([P, 16], F32, name="negm")
-            c0 = 8 * kind + 4 * half
-            negs = small.tile([P, 16], F32, name="negs")
-            nc.gpsimd.tensor_scalar(
-                out=negs[:],
-                in0=S[p]["su"][:],
-                scalar1=-1.0 / 128.0,
-                scalar2=0.0,
-                op0=ALU.mult,
-                op1=ALU.add,
-            )
-            nc.gpsimd.tensor_tensor(
-                out=negm[:].rearrange("q (i n) -> q i n", n=4),
-                in0=negs[:].rearrange("q (i n) -> q i n", n=4),
-                in1=nsb[:, c0 : c0 + 4].unsqueeze(1).to_broadcast([P, 4, 4]),
-                op=ALU.add,
+            nc.scalar.activation(
+                out=negm[:], in_=S[p]["su"][:], func=ACT.Identity, scale=-1.0 / 128.0
             )
             S[p]["negm"] = negm
 
@@ -347,39 +332,39 @@ def tile_axialattentionblock_pa_kernel(
         x_small(0)
         w_turn(Q0)
         x_scale(0, 0)
-        w_quant(Q0, 0)
-        x_quant(0, 0)
+        centre()
+        w_quant(Q0, 0, 1)
+        x_quant(0, 0, 1)
         x_scale(0, 1)
-        w_quant(Q0, 1)
-        x_quant(0, 1)
+        w_quant(Q0, 1, 2)
+        x_quant(0, 1, 2)
+        qk_vectors(Q0)
         w_turn(K0)
-        bias_sums()
-        w_quant(K0, 0)
-        w_quant(K0, 1)
+        ln_vectors()
+        w_quant(K0, 0, 2)
         w_turn(Q1)
 
         def filler(p):
             if p == 0:
+                qk_vectors(K0)
                 w_turn(K1)
-                w_quant(Q1, 0)
-                w_quant(Q1, 1)
+                w_quant(Q1, 0, 2)
                 x_stats(1)
-                x_small(1)
             elif p == 1:
+                x_small(1)
+                qk_vectors(Q1)
+                qk_vectors(K1)
                 w_turn(V0)
                 x_scale(1, 0)
-                w_quant(K1, 0)
-                w_quant(K1, 1)
-                x_quant(1, 0)
+                w_quant(K1, 0, 2)
+                v_vectors()
             elif p == 2:
                 w_turn(V1)
                 x_scale(1, 1)
-                w_quant(V0, 0)
-                w_quant(V0, 1)
-                x_quant(1, 1)
+                x_quant(1, 0, 2)
+                w_quant(V0, 0, 2)
             elif p == 3:
-                w_quant(V1, 0)
-                w_quant(V1, 1)
+                w_quant(V1, 0, 2)
                 v_unit(V0, 0)
             elif p == 4:
                 v_unit(V1, 0)

@@ -35,8 +35,8 @@ def tile_axialattentionblock_pa_kernel(
         vp = ctx.enter_context(tc.tile_pool(name="vp", bufs=2))
         jp = ctx.enter_context(tc.tile_pool(name="jp", bufs=2))
         psc = ctx.enter_context(tc.psum_pool(name="psc", bufs=1))
-        psx = ctx.enter_context(tc.psum_pool(name="psx", bufs=4))
-        psa = ctx.enter_context(tc.psum_pool(name="psa", bufs=3))
+        psx = ctx.enter_context(tc.psum_pool(name="psx", bufs=5))
+        psa = ctx.enter_context(tc.psum_pool(name="psa", bufs=2))
 
         x_sb = const.tile([P, 2, 2, 2048], BF16, name="x_sb")
         w_view = qkv_w.rearrange("(n t p) k -> t p n k", t=3, p=P)
@@ -95,7 +95,13 @@ def tile_axialattentionblock_pa_kernel(
             )
 
         lnc = psc.tile([P, 512], F32, name="lnc")
-        b_qk = const.tile([P, 2, 8, P], F32, name="b_qk")
+        b_qk = const.tile([P, 1, 8, P], F32, name="b_qk")
+        bcol = const.tile([P, 24], F32, name="bcol")
+        lnk = const.tile([P, 2, P], F32, name="lnk")
+        cmat = const.tile([P, P], F32, name="cmat")
+        nc.gpsimd.tensor_scalar(
+            out=cmat[:], in0=ident[:], scalar1=1.0, scalar2=-1.0 / 128.0, op0=ALU.mult, op1=ALU.add
+        )
         b_v = const.tile([P, 8, P], F32, name="b_v")
 
         vecm = const.tile([P, P], F32, name="vecm")
@@ -110,6 +116,10 @@ def tile_axialattentionblock_pa_kernel(
         def ln_vectors():
             for k in range(4):
                 spread(lnc[:, P * k : P * (k + 1)], ident_b, 24 + k, vec)
+            nc.scalar.copy(out=lnk[:], in_=lnc[:].rearrange("q (a k c) -> q a k c", a=2, k=2)[:, :, 1, :])
+            bt = psx.tile([P, P], F32, tag="aux", name="bt")
+            nc.tensor.matmul(out=bt[:], lhsT=vec[:], rhs=ident_b[:], start=True, stop=True)
+            nc.scalar.copy(out=bcol[:], in_=bt[:, 0:24])
 
         def qk_vectors(chunk):
             kind, h = chunk
@@ -131,24 +141,33 @@ def tile_axialattentionblock_pa_kernel(
         hc = {}
         hs = {}
 
-        mv = const.tile([P, 2, 8, 2], F32, name="mv")
-
         def x_stats(b):
             for s in range(8):
                 g, t = divmod(s, 4)
                 nc.vector.bn_stats(out=st[:, b, s, :], in_=x_sb[:, b, g, 512 * t : 512 * (t + 1)])
-            for s in range(8):
-                nc.vector.bn_aggr(out=mv[:, b, s, :], in_=st[:, b, s, :])
 
         def x_small(b):
+            eng = nc.vector if b == 0 else nc.gpsimd
+            d = small.tile([P, 8], F32, name="xd")
+            eng.tensor_tensor(out=d[:], in0=st[:, b, :, 1], in1=st[:, b, :, 4], op=ALU.subtract)
+            m2 = small.tile([P, 8], F32, name="xm2")
+            eng.tensor_tensor(out=m2[:], in0=st[:, b, :, 2], in1=st[:, b, :, 5], op=ALU.add)
+            d2 = small.tile([P, 8], F32, name="xd2")
+            eng.tensor_tensor(out=d2[:], in0=d[:], in1=d[:], op=ALU.mult)
+            d3 = small.tile([P, 8], F32, name="xd3")
+            eng.tensor_scalar(
+                out=d3[:], in0=d2[:], scalar1=128.0, scalar2=0.0, op0=ALU.mult, op1=ALU.add
+            )
+            ss = small.tile([P, 8], F32, name="xss")
+            eng.tensor_tensor(out=ss[:], in0=d3[:], in1=m2[:], op=ALU.add)
             sd = small.tile([P, 8], F32, name="xsd")
-            nc.scalar.activation(out=sd[:], in_=mv[:, b, :, 1], func=ACT.Sqrt, scale=512.0 / 511.0)
+            nc.scalar.activation(out=sd[:], in_=ss[:], func=ACT.Sqrt, scale=1.0 / 511.0)
             den = small.tile([P, 8], F32, name="xden")
-            nc.vector.tensor_scalar_add(out=den[:], in0=sd[:], scalar1=1e-8)
+            eng.tensor_scalar_add(out=den[:], in0=sd[:], scalar1=1e-8)
             rec = small.tile([P, 8], F32, name="xrec")
             nc.vector.reciprocal(out=rec[:], in_=den[:])
             sc = small.tile([P, 8], F32, name="xsc")
-            nc.vector.tensor_tensor(out=sc[:], in0=rec[:], in1=nw[:], op=ALU.mult)
+            eng.tensor_tensor(out=sc[:], in0=rec[:], in1=nw[:], op=ALU.mult)
             xsc[b] = sc
 
         def x_scale(b, g):
@@ -282,9 +301,11 @@ def tile_axialattentionblock_pa_kernel(
                         bias=negm[:, k : k + 1],
                         accum_out=ssq[:, k : k + 1],
                     )
-            sd = small.tile([P, 16], F32, name="sd")
-            nc.scalar.activation(out=sd[:], in_=ssq[:], func=ACT.Sqrt, bias=eps[:], scale=1.0 / 128.0)
-            S[p]["sd"] = sd
+            rs = small.tile([P, 16], F32, name="rs")
+            nc.scalar.activation(
+                out=rs[:], in_=ssq[:], func=ACT.Abs_reciprocal_sqrt, bias=eps[:], scale=1.0 / 128.0
+            )
+            S[p]["rs"] = rs
 
         def stage_mv(p):
             (kind, half), b = QK_UNITS[p]
@@ -307,8 +328,7 @@ def tile_axialattentionblock_pa_kernel(
             chunk, b = QK_UNITS[p]
             kind, half = chunk
             ost = S[p]["ost"]
-            rs = small.tile([P, 16], F32, name="rs")
-            nc.vector.reciprocal(out=rs[:], in_=S[p]["sd"][:])
+            rs = S[p]["rs"]
             for n in range(4):
                 for i in range(4):
                     k = 4 * i + n
@@ -328,6 +348,73 @@ def tile_axialattentionblock_pa_kernel(
             if not by_head:
                 store(chunk, b, ost)
 
+        def k_exit(p):
+            chunk, b = QK_UNITS[p]
+            kind, half = chunk
+            zs = []
+            for n in range(4):
+                acc = psa.tile([P, 512], F32, name="acc")
+                for g in range(2):
+                    nc.tensor.matmul_mx(
+                        out=acc[:],
+                        lhsT=wc[chunk][:, g, P * n : P * (n + 1)].bitcast(FP8X4),
+                        lhsT_scale=ws[chunk][:, g, P * n : P * (n + 1)],
+                        rhs=hc[b][:, g, :].bitcast(FP8X4),
+                        rhs_scale=hs[b][:, g, :],
+                        start=(g == 0),
+                        stop=(g == 1),
+                    )
+                z = zp.tile([P, 512], F32, name="z")
+                col = 3 * (4 * half + n) + kind
+                nc.scalar.activation(
+                    out=z[:], in_=acc[:], func=ACT.Identity, bias=bcol[:, col : col + 1]
+                )
+                zs.append(z)
+            S[p] = {"zs": zs, "d": {}, "ost": op.tile([P, 4, 4, P], F32, name="ost")}
+
+        def k_turn(p, n):
+            z = S[p]["zs"][n]
+            d = psx.tile([P, 4, P], F32, tag="aux", name="d")
+            for i in range(4):
+                nc.tensor.matmul(
+                    out=d[:, i, :], lhsT=z[:, P * i : P * (i + 1)], rhs=cmat[:], start=True, stop=True
+                )
+            ssq = small.tile([P, 4], F32, name="ssqk")
+            for i in range(4):
+                junk = jp.tile([P, P], F32, name="junk")
+                nc.scalar.activation(
+                    out=junk[:], in_=d[:, i, :], func=ACT.Square, accum_out=ssq[:, i : i + 1]
+                )
+            rs = small.tile([P, 4], F32, name="rsk")
+            nc.scalar.activation(
+                out=rs[:], in_=ssq[:], func=ACT.Abs_reciprocal_sqrt, bias=eps[:], scale=1.0 / 128.0
+            )
+            S[p]["d"][n] = (d, rs)
+
+        def k_out(p, n):
+            chunk, b = QK_UNITS[p]
+            (d, rs), ost = S[p]["d"][n], S[p]["ost"]
+            for i in range(4):
+                nc.vector.scalar_tensor_tensor(
+                    out=ost[:, n, i, :],
+                    in0=d[:, i, :],
+                    scalar=rs[:, i : i + 1],
+                    in1=lnk[:, 0, :],
+                    op0=ALU.mult,
+                    op1=ALU.mult,
+                )
+            eng = nc.vector if p == 7 else nc.gpsimd
+            eng.tensor_tensor(
+                out=ost[:, n, :, :],
+                in0=ost[:, n, :, :],
+                in1=lnk[:, 1, :].unsqueeze(1).to_broadcast([P, 4, P]),
+                op=ALU.add,
+            )
+            nc.sync.dma_start(
+                out=outs[1][b, 4 * chunk[1] + n].rearrange("h (w i) c -> (h w) (i c)", i=4),
+                in_=ost[:, n].rearrange("q i c -> q (i c)"),
+            )
+
         x_stats(0)
         x_small(0)
         w_turn(Q0)
@@ -346,14 +433,12 @@ def tile_axialattentionblock_pa_kernel(
 
         def filler(p):
             if p == 0:
-                qk_vectors(K0)
                 w_turn(K1)
                 w_quant(Q1, 0, 2)
                 x_stats(1)
             elif p == 1:
                 x_small(1)
                 qk_vectors(Q1)
-                qk_vectors(K1)
                 w_turn(V0)
                 x_scale(1, 0)
                 w_quant(K1, 0, 2)
@@ -373,14 +458,30 @@ def tile_axialattentionblock_pa_kernel(
             elif p == 6:
                 v_unit(V1, 1)
 
+        def is_q(p):
+            return 0 <= p < 8 and QK_UNITS[p][0][0] == 0
+
+        def is_k(p):
+            return 0 <= p < 8 and QK_UNITS[p][0][0] == 1
+
         for p in range(10):
-            if p < 8:
+            if is_q(p):
                 stage_e(p)
-            if 0 <= p - 2 < 8:
-                stage_f(p - 2, p - 2 == 7)
-            if 0 <= p - 1 < 8:
+            if is_k(p):
+                k_exit(p)
+            if is_q(p - 2):
+                stage_f(p - 2, False)
+            if is_k(p - 1):
+                k_turn(p - 1, 0)
+                k_turn(p - 1, 1)
+            if is_q(p - 1):
                 stage_mv(p - 1)
                 stage_ms(p - 1)
-            if p < 8:
+            if is_k(p - 1):
+                for n in range(4):
+                    k_out(p - 1, n)
+                    if n < 2:
+                        k_turn(p - 1, n + 2)
+            if is_q(p):
                 stage_n(p)
             filler(p)

from contextlib import ExitStack

import concourse.masks as masks
import concourse.mybir as mybir

F32 = mybir.dt.float32
BF16 = mybir.dt.bfloat16
U32 = mybir.dt.uint32
U8 = mybir.dt.uint8
I32 = mybir.dt.int32
FP8X4 = mybir.dt.float8_e4m3fn_x4
ALU = mybir.AluOpType
ACT = mybir.ActivationFunctionType

P = 128
FLOPS = 2 * 3072 * 1024 * 1024

Q0, K0, Q1, K1, V0, V1 = (0, 0), (1, 0), (0, 1), (1, 1), (2, 0), (2, 1)
LOAD_ORDER = (Q0, K0, Q1, K1, V0, V1)
QK_UNITS = ((Q0, 0), (K0, 0), (Q1, 0), (K1, 0), (Q0, 1), (K0, 1), (Q1, 1), (K1, 1))


def tile_axialattentionblock_pa_kernel(
    tc, x, norm1_w, qkv_w, qkv_b, qn_w, qn_b, kn_w, kn_b, out_0, out_1, out_2
):
    nc = tc.nc
    outs = (out_0, out_1, out_2)
    with ExitStack() as ctx:
        const = ctx.enter_context(tc.tile_pool(name="const", bufs=1))
        wgp = ctx.enter_context(tc.tile_pool(name="wgp", bufs=3))
        hgp = ctx.enter_context(tc.tile_pool(name="hgp", bufs=2))
        small = ctx.enter_context(tc.tile_pool(name="small", bufs=4))
        zp = ctx.enter_context(tc.tile_pool(name="zp", bufs=12))
        op = ctx.enter_context(tc.tile_pool(name="op", bufs=3))
        vp = ctx.enter_context(tc.tile_pool(name="vp", bufs=2))
        jp = ctx.enter_context(tc.tile_pool(name="jp", bufs=2))
        psc = ctx.enter_context(tc.psum_pool(name="psc", bufs=1))
        psx = ctx.enter_context(tc.psum_pool(name="psx", bufs=5))
        psa = ctx.enter_context(tc.psum_pool(name="psa", bufs=2))

        x_sb = const.tile([P, 2, 2, 2048], BF16, name="x_sb")
        w_view = qkv_w.rearrange("(n t p) k -> t p n k", t=3, p=P)
        wraw = {}

        def load_x(b, g, lo, hi):
            nc.sync.dma_start(
                out=x_sb[:, b, g, 512 * lo : 512 * hi],
                in_=x[b].rearrange("(g q t) h w -> g q (t h w)", g=2, t=4)[g][:, 512 * lo : 512 * hi],
            )

        def load_w(chunk):
            kind, half = chunk
            wr = const.tile([P, 4, 1024], BF16, name="wraw%d%d" % chunk)
            nc.sync.dma_start(out=wr[:], in_=w_view[kind, :, 4 * half : 4 * half + 4, :])
            wraw[chunk] = wr

        for g in range(2):
            for lo in (0, 2):
                load_x(0, g, lo, lo + 2)
        load_w(Q0)
        load_w(K0)
        load_w(Q1)
        load_w(K1)
        load_x(1, 0, 0, 4)
        load_x(1, 1, 0, 4)
        load_w(V0)
        load_w(V1)

        one1 = const.tile([P, 1], F32, name="one1")
        nc.vector.memset(one1[:], 1.0)
        eps = const.tile([P, 1], F32, name="eps")
        nc.vector.memset(eps[:], 1e-5)
        warm = const.tile([P, 1], F32, name="warm")
        nc.scalar.activation(out=warm[:], in_=one1[:], func=ACT.Sqrt)
        vec = const.tile([P, P], BF16, name="vec")
        nc.vector.memset(vec[:].bitcast(I32), 0)
        nc.scalar.dma_start(out=vec[0:24, :], in_=qkv_b.rearrange("(r c) -> r c", c=P))
        for r, v in enumerate((qn_w, kn_w, qn_b, kn_b)):
            nc.scalar.dma_start(out=vec[24 + r : 25 + r, :], in_=v.rearrange("(o n) -> o n", o=1))
        nw = const.tile([P, 8], BF16, name="nw")
        with nc.allow_non_contiguous_dma(reason="1024 gains, four to a piece"):
            nc.scalar.dma_start(
                out=nw[:].rearrange("q (g t) -> q g t", t=4),
                in_=norm1_w.rearrange("(g q t) -> q g t", g=2, t=4),
            )

        ident = const.tile([P, P], F32, name="ident")
        masks.make_identity(nc, ident[:])
        ident_b = const.tile([P, P], BF16, name="ident_b")
        nc.gpsimd.tensor_copy(out=ident_b[:], in_=ident[:])

        def spread(out, eye, r, rows):
            nc.tensor.matmul(
                out=out, lhsT=eye[:, r : r + 1].to_broadcast([P, P]), rhs=rows[:], start=True, stop=True
            )

        lnc = psc.tile([P, 512], F32, name="lnc")
        b_qk = const.tile([P, 1, 8, P], F32, name="b_qk")
        bcol = const.tile([P, 24], F32, name="bcol")
        lnk = const.tile([P, 2, P], F32, name="lnk")
        cmat = const.tile([P, P], F32, name="cmat")
        nc.gpsimd.tensor_scalar(
            out=cmat[:], in0=ident[:], scalar1=1.0, scalar2=-1.0 / 128.0, op0=ALU.mult, op1=ALU.add
        )
        b_v = const.tile([P, 8, P], F32, name="b_v")

        vecm = const.tile([P, P], F32, name="vecm")

        def centre():
            rowsum = small.tile([P, 1], F32, name="rowsum")
            nc.vector.reduce_sum(out=rowsum[:], in_=vec[:], axis=mybir.AxisListType.X)
            rowmean = small.tile([P, 1], F32, name="rowmean")
            nc.vector.tensor_scalar_mul(out=rowmean[:], in0=rowsum[:], scalar1=-1.0 / 128.0)
            nc.vector.tensor_scalar_add(out=vecm[:], in0=vec[:], scalar1=rowmean[:])

        def ln_vectors():
            for k in range(4):
                spread(lnc[:, P * k : P * (k + 1)], ident_b, 24 + k, vec)
            nc.scalar.copy(out=lnk[:], in_=lnc[:].rearrange("q (a k c) -> q a k c", a=2, k=2)[:, :, 1, :])
            bt = psx.tile([P, P], F32, tag="aux", name="bt")
            nc.tensor.matmul(out=bt[:], lhsT=vec[:], rhs=ident_b[:], start=True, stop=True)
            nc.scalar.copy(out=bcol[:], in_=bt[:, 0:24])

        def qk_vectors(chunk):
            kind, h = chunk
            qb = psx.tile([P, 4, P], F32, tag="aux", name="qb")
            for n in range(4):
                spread(qb[:, n, :], ident, 3 * (4 * h + n) + kind, vecm)
            nc.scalar.copy(out=b_qk[:, kind, 4 * h : 4 * h + 4, :], in_=qb[:])

        def v_vectors():
            for h in range(2):
                vb = psx.tile([P, 4, P], F32, tag="aux", name="vb")
                for n in range(4):
                    spread(vb[:, n, :], ident_b, 3 * (4 * h + n) + 2, vec)
                nc.scalar.copy(out=b_v[:, 4 * h : 4 * h + 4, :], in_=vb[:])

        st = const.tile([P, 2, 8, 6], F32, name="st")
        xsc = {}
        hgs = {}
        hc = {}
        hs = {}

        def x_stats(b):
            for s in range(8):
                g, t = divmod(s, 4)
                nc.vector.bn_stats(out=st[:, b, s, :], in_=x_sb[:, b, g, 512 * t : 512 * (t + 1)])

        def x_small(b):
            eng = nc.vector if b == 0 else nc.gpsimd
            d = small.tile([P, 8], F32, name="xd")
            eng.tensor_tensor(out=d[:], in0=st[:, b, :, 1], in1=st[:, b, :, 4], op=ALU.subtract)
            m2 = small.tile([P, 8], F32, name="xm2")
            eng.tensor_tensor(out=m2[:], in0=st[:, b, :, 2], in1=st[:, b, :, 5], op=ALU.add)
            d2 = small.tile([P, 8], F32, name="xd2")
            eng.tensor_tensor(out=d2[:], in0=d[:], in1=d[:], op=ALU.mult)
            d3 = small.tile([P, 8], F32, name="xd3")
            eng.tensor_scalar(
                out=d3[:], in0=d2[:], scalar1=128.0, scalar2=0.0, op0=ALU.mult, op1=ALU.add
            )
            ss = small.tile([P, 8], F32, name="xss")
            eng.tensor_tensor(out=ss[:], in0=d3[:], in1=m2[:], op=ALU.add)
            sd = small.tile([P, 8], F32, name="xsd")
            nc.scalar.activation(out=sd[:], in_=ss[:], func=ACT.Sqrt, scale=1.0 / 511.0)
            den = small.tile([P, 8], F32, name="xden")
            eng.tensor_scalar_add(out=den[:], in0=sd[:], scalar1=1e-8)
            rec = small.tile([P, 8], F32, name="xrec")
            nc.vector.reciprocal(out=rec[:], in_=den[:])
            sc = small.tile([P, 8], F32, name="xsc")
            eng.tensor_tensor(out=sc[:], in0=rec[:], in1=nw[:], op=ALU.mult)
            xsc[b] = sc

        def x_scale(b, g):
            if g == 0:
                hgs[b] = hgp.tile([P, 2, 2048], BF16, name="hg", align_bytes=64)
                hc[b] = const.tile([P, 2, 512], U32, name="hc%d" % b, align_bytes=64)
                hs[b] = const.tile([P, 2, 512], U8, name="hs%d" % b, align_bytes=64)
            nc.vector.tensor_tensor(
                out=hgs[b][:, g, :].rearrange("q (i p t) -> q i p t", i=4, t=4),
                in0=x_sb[:, b, g, :].rearrange("q (t p i) -> q i p t", t=4, i=4),
                in1=xsc[b][:, 4 * g : 4 * g + 4].unsqueeze(1).unsqueeze(1).to_broadcast([P, 4, P, 4]),
                op=ALU.mult,
            )

        def quant(codes, scales, grouped, lo, hi):
            nc.vector.quantize_mx(
                out=codes[:, lo:hi, :].rearrange("q g w -> q (g w)").bitcast(FP8X4),
                scales=scales[:, lo:hi, :].rearrange("q g w -> q (g w)"),
                in_=grouped[:, lo:hi, :].rearrange("q g w -> q (g w)"),
            )

        def x_quant(b, lo, hi):
            quant(hc[b], hs[b], hgs[b], lo, hi)

        wgs = {}
        wc = {}
        ws = {}

        def w_turn(chunk):
            wrf = wraw[chunk][:].bitcast(F32)
            wg = wgp.tile([P, 2, 2048], BF16, name="wg", align_bytes=64)
            wgf = wg[:].bitcast(F32)
            for g in range(2):
                for h in range(2):
                    tp = psx.tile([P, 2, 2, P], F32, tag="aux", name="tp")
                    for u in range(2):
                        for nn in range(2):
                            c0 = 2 * P * g + u
                            nc.tensor.transpose(
                                out=tp[:, u, nn, :],
                                in_=wrf[:, 2 * h + nn, c0 : 2 * P * (g + 1) : 2],
                                identity=ident[:],
                            )
                    nc.scalar.copy(
                        out=wgf[:, g, 512 * h : 512 * (h + 1)].rearrange("q (o u) -> q o u", u=2),
                        in_=tp[:].rearrange("q u n p -> q (n p) u"),
                    )
            wgs[chunk] = wg
            wc[chunk] = const.tile([P, 2, 512], U32, name="wc%d%d" % chunk, align_bytes=64)
            ws[chunk] = const.tile([P, 2, 512], U8, name="ws%d%d" % chunk, align_bytes=64)

        def w_quant(chunk, lo, hi):
            quant(wc[chunk], ws[chunk], wgs[chunk], lo, hi)

        def product(acc, chunk, b, i):
            for g in range(2):
                nc.tensor.matmul_mx(
                    out=acc[:],
                    lhsT=hc[b][:, g, P * i : P * (i + 1)].bitcast(FP8X4),
                    lhsT_scale=hs[b][:, g, P * i : P * (i + 1)],
                    rhs=wc[chunk][:, g, :].bitcast(FP8X4),
                    rhs_scale=ws[chunk][:, g, :],
                    start=(g == 0),
                    stop=(g == 1),
                )

        def store(chunk, b, tile_):
            kind, half = chunk
            nc.sync.dma_start(
                out=outs[kind][b, 4 * half : 4 * half + 4].rearrange("n h (w i) c -> (h w) n (i c)", i=4),
                in_=tile_[:].rearrange("q n i c -> q n (i c)"),
            )

        def v_unit(chunk, b):
            vst = vp.tile([P, 4, 4, P], F32, name="vst")
            for i in range(4):
                acc = psx.tile([P, 512], F32, tag="aux", name="vacc")
                product(acc, chunk, b, i)
                nc.vector.tensor_tensor(
                    out=vst[:, :, i, :],
                    in0=acc[:].rearrange("q (n c) -> q n c", c=P),
                    in1=b_v[:, 4 * chunk[1] : 4 * chunk[1] + 4, :],
                    op=ALU.add,
                )
            store(chunk, b, vst)

        S = {}

        def stage_e(p):
            chunk, b = QK_UNITS[p]
            su = small.tile([P, 16], F32, name="su")
            zs = []
            for i in range(4):
                acc = psa.tile([P, 512], F32, name="acc")
                product(acc, chunk, b, i)
                z = zp.tile([P, 512], F32, name="z")
                for n in range(4):
                    nc.scalar.activation(
                        out=z[:, P * n : P * (n + 1)],
                        in_=acc[:, P * n : P * (n + 1)],
                        func=ACT.Identity,
                        accum_out=su[:, 4 * i + n : 4 * i + n + 1],
                    )
                nc.gpsimd.tensor_tensor(
                    out=z[:].rearrange("q (n c) -> q n c", c=P),
                    in0=z[:].rearrange("q (n c) -> q n c", c=P),
                    in1=b_qk[:, chunk[0], 4 * chunk[1] : 4 * chunk[1] + 4, :],
                    op=ALU.add,
                )
                zs.append(z)
            S[p] = {"su": su, "zs": zs}

        def stage_n(p):
            negm = small.tile([P, 16], F32, name="negm")
            nc.scalar.activation(
                out=negm[:], in_=S[p]["su"][:], func=ACT.Identity, scale=-1.0 / 128.0
            )
            S[p]["negm"] = negm

        def stage_ms(p):
            negm = S[p]["negm"]
            ssq = small.tile([P, 16], F32, name="ssq")
            for i in range(4):
                for n in range(4):
                    k = 4 * i + n
                    junk = jp.tile([P, P], F32, name="junk")
                    nc.scalar.activation(
                        out=junk[:],
                        in_=S[p]["zs"][i][:, P * n : P * (n + 1)],
                        func=ACT.Square,
                        bias=negm[:, k : k + 1],
                        accum_out=ssq[:, k : k + 1],
                    )
            rs = small.tile([P, 16], F32, name="rs")
            nc.scalar.activation(
                out=rs[:], in_=ssq[:], func=ACT.Abs_reciprocal_sqrt, bias=eps[:], scale=1.0 / 128.0
            )
            S[p]["rs"] = rs

        def stage_mv(p):
            (kind, half), b = QK_UNITS[p]
            negm = S[p]["negm"]
            ost = op.tile([P, 4, 4, P], F32, name="ost")
            for i in range(4):
                for n in range(4):
                    k = 4 * i + n
                    nc.vector.scalar_tensor_tensor(
                        out=ost[:, n, i, :],
                        in0=S[p]["zs"][i][:, P * n : P * (n + 1)],
                        scalar=negm[:, k : k + 1],
                        in1=lnc[:, P * kind : P * (kind + 1)],
                        op0=ALU.add,
                        op1=ALU.mult,
                    )
            S[p]["ost"] = ost

        def stage_f(p, by_head):
            chunk, b = QK_UNITS[p]
            kind, half = chunk
            ost = S[p]["ost"]
            rs = S[p]["rs"]
            for n in range(4):
                for i in range(4):
                    k = 4 * i + n
                    nc.vector.scalar_tensor_tensor(
                        out=ost[:, n, i, :],
                        in0=ost[:, n, i, :],
                        scalar=rs[:, k : k + 1],
                        in1=lnc[:, 256 + P * kind : 256 + P * (kind + 1)],
                        op0=ALU.mult,
                        op1=ALU.add,
                    )
                if by_head:
                    nc.sync.dma_start(
                        out=outs[kind][b, 4 * half + n].rearrange("h (w i) c -> (h w) (i c)", i=4),
                        in_=ost[:, n].rearrange("q i c -> q (i c)"),
                    )
            if not by_head:
                store(chunk, b, ost)

        def k_exit(p):
            chunk, b = QK_UNITS[p]
            kind, half = chunk
            zs = []
            for n in range(4):
                acc = psa.tile([P, 512], F32, name="acc")
                for g in range(2):
                    nc.tensor.matmul_mx(
                        out=acc[:],
                        lhsT=wc[chunk][:, g, P * n : P * (n + 1)].bitcast(FP8X4),
                        lhsT_scale=ws[chunk][:, g, P * n : P * (n + 1)],
                        rhs=hc[b][:, g, :].bitcast(FP8X4),
                        rhs_scale=hs[b][:, g, :],
                        start=(g == 0),
                        stop=(g == 1),
                    )
                z = zp.tile([P, 512], F32, name="z")
                col = 3 * (4 * half + n) + kind
                nc.scalar.activation(
                    out=z[:], in_=acc[:], func=ACT.Identity, bias=bcol[:, col : col + 1]
                )
                zs.append(z)
            S[p] = {"zs": zs, "d": {}, "ost": op.tile([P, 4, 4, P], F32, name="ost")}

        def k_turn(p, n):
            z = S[p]["zs"][n]
            d = psx.tile([P, 4, P], F32, tag="aux", name="d")
            for i in range(4):
                nc.tensor.matmul(
                    out=d[:, i, :], lhsT=z[:, P * i : P * (i + 1)], rhs=cmat[:], start=True, stop=True
                )
            ssq = small.tile([P, 4], F32, name="ssqk")
            for i in range(4):
                junk = jp.tile([P, P], F32, name="junk")
                nc.scalar.activation(
                    out=junk[:], in_=d[:, i, :], func=ACT.Square, accum_out=ssq[:, i : i + 1]
                )
            rs = small.tile([P, 4], F32, name="rsk")
            nc.scalar.activation(
                out=rs[:], in_=ssq[:], func=ACT.Abs_reciprocal_sqrt, bias=eps[:], scale=1.0 / 128.0
            )
            S[p]["d"][n] = (d, rs)

        def k_out(p, n):
            chunk, b = QK_UNITS[p]
            (d, rs), ost = S[p]["d"][n], S[p]["ost"]
            for i in range(4):
                nc.vector.scalar_tensor_tensor(
                    out=ost[:, n, i, :],
                    in0=d[:, i, :],
                    scalar=rs[:, i : i + 1],
                    in1=lnk[:, 0, :],
                    op0=ALU.mult,
                    op1=ALU.mult,
                )
            eng = nc.vector if p == 7 else nc.gpsimd
            eng.tensor_tensor(
                out=ost[:, n, :, :],
                in0=ost[:, n, :, :],
                in1=lnk[:, 1, :].unsqueeze(1).to_broadcast([P, 4, P]),
                op=ALU.add,
            )
            nc.sync.dma_start(
                out=outs[1][b, 4 * chunk[1] + n].rearrange("h (w i) c -> (h w) (i c)", i=4),
                in_=ost[:, n].rearrange("q i c -> q (i c)"),
            )

        x_stats(0)
        x_small(0)
        w_turn(Q0)
        x_scale(0, 0)
        centre()
        w_quant(Q0, 0, 1)
        x_quant(0, 0, 1)
        x_scale(0, 1)
        w_quant(Q0, 1, 2)
        x_quant(0, 1, 2)
        qk_vectors(Q0)
        w_turn(K0)
        ln_vectors()
        w_quant(K0, 0, 2)
        w_turn(Q1)

        def filler(p):
            if p == 0:
                w_turn(K1)
                w_quant(Q1, 0, 2)
                x_stats(1)
            elif p == 1:
                x_small(1)
                qk_vectors(Q1)
                w_turn(V0)
                x_scale(1, 0)
                w_quant(K1, 0, 2)
                v_vectors()
            elif p == 2:
                w_turn(V1)
                x_scale(1, 1)
                x_quant(1, 0, 2)
                w_quant(V0, 0, 2)
            elif p == 3:
                w_quant(V1, 0, 2)
                v_unit(V0, 0)
            elif p == 4:
                v_unit(V1, 0)
            elif p == 5:
                v_unit(V0, 1)
            elif p == 6:
                v_unit(V1, 1)

        def is_q(p):
            return 0 <= p < 8 and QK_UNITS[p][0][0] == 0

        def is_k(p):
            return 0 <= p < 8 and QK_UNITS[p][0][0] == 1

        for p in range(10):
            if is_q(p):
                stage_e(p)
            if is_k(p):
                k_exit(p)
            if is_q(p - 2):
                stage_f(p - 2, False)
            if is_k(p - 1):
                k_turn(p - 1, 0)
                k_turn(p - 1, 1)
            if is_q(p - 1):
                stage_mv(p - 1)
                stage_ms(p - 1)
            if is_k(p - 1):
                for n in range(4):
                    k_out(p - 1, n)
                    if n < 2:
                        k_turn(p - 1, n + 2)
            if is_q(p):
                stage_n(p)
            filler(p)
